import numpy as np
import ml_dtypes

BF16 = ml_dtypes.bfloat16


def bf(x):
    return np.asarray(x, np.float32).astype(BF16)


def f32(x):
    return np.asarray(x, np.float32)


def f64(x):
    return np.asarray(x).astype(np.float64)


def striped(idx):
    return np.tile(idx.reshape(-1, 16).T, (8, 1))


E, S, N, H, D, MW = 128, 256, 256, 2, 128, 256


def setup_inputs():
    return {
        "x": bf(np.random.standard_normal((E, S))),
        "wq": bf(np.random.standard_normal((E, H * D)) / np.sqrt(E)),
        "bq": f32(0.1 * np.random.standard_normal((H * D, 1))),
        "key_params": f32(1.25 * np.random.standard_normal((H * D, MW))),
        "calibration": f32(0.5 * np.random.standard_normal((H * D, MW))),
        "value": bf(5.0 * (2.0 * np.random.random_sample((H * MW, E)) - 1.0)),
        "bd": f32(0.1 * np.random.standard_normal((E, 1))),
        "offs": striped(np.random.permutation(S)[:N]),
    }


def reference(x, wq, bq, key_params, calibration, value, bd, offs):
    idx = offs[:16].T.reshape(-1)
    q = f64(wq).T @ f64(x)[:, idx] + f64(bq)
    k = f64(key_params) + f64(calibration)
    v = f64(value)
    res = np.zeros((E, idx.size)) + f64(bd)
    for h in range(H):
        score = k[h * D:(h + 1) * D].T @ q[h * D:(h + 1) * D] / np.sqrt(E)
        e = np.exp(score)
        attn = e / e.sum(axis=0, keepdims=True)
        res = res + v[h * MW:(h + 1) * MW].T @ attn
    return res

@@ -1,0 +1,104 @@
+import math
+
+import concourse.mybir as mybir
+from concourse.masks import make_identity
+
+BF16, F32, U16 = mybir.dt.bfloat16, mybir.dt.float32, mybir.dt.uint16
+ADD, MULT, MAX = mybir.AluOpType.add, mybir.AluOpType.mult, mybir.AluOpType.max
+EXP = mybir.ActivationFunctionType.Exp
+
+P = 128
+E, S, N, H, D, MW = 128, 256, 256, 2, 128, 256
+JB = N // P
+MB = MW // P
+SCALE = 1.0 / math.sqrt(E)
+
+FLOPS = 2 * E * H * D * N + 2 * H * D * MW * N + 2 * H * MW * E * N
+
+
+def tile_autocalibrationinjector_kernel(tc, x, wq, bq, key_params, calibration, value, bd, offs, out):
+    nc = tc.nc
+    with (
+        tc.tile_pool(name="held", bufs=1) as held,
+        tc.psum_pool(name="psum", bufs=1) as psum,
+    ):
+        offsets = held.tile([P, N // 16], U16, name="offsets")
+        nc.sync.dma_start(offsets[:], offs)
+        x_sb = held.tile([E, S], BF16, name="x_sb")
+        nc.sync.dma_start(x_sb[:], x)
+        wq_sb = held.tile([E, H * D], BF16, name="wq_sb")
+        nc.scalar.dma_start(wq_sb[:], wq)
+        bq_sb = [held.tile([D, 1], F32, name=f"bq_sb{h}") for h in range(H)]
+        for h in range(H):
+            nc.scalar.dma_start(bq_sb[h][:], bq[h * D : (h + 1) * D, :])
+        key_sb = [held.tile([D, MW], F32, name=f"key_sb{h}") for h in range(H)]
+        cal_sb = [held.tile([D, MW], F32, name=f"cal_sb{h}") for h in range(H)]
+        for h in range(H):
+            nc.sync.dma_start(key_sb[h][:], key_params[h * D : (h + 1) * D, :])
+            nc.scalar.dma_start(cal_sb[h][:], calibration[h * D : (h + 1) * D, :])
+        value_sb = held.tile([P, H * MB, E], BF16, name="value_sb")
+        nc.gpsimd.dma_start(value_sb[:], value.rearrange("(c m) e -> m c e", m=P))
+        bd_sb = held.tile([E, 1], F32, name="bd_sb")
+        nc.gpsimd.dma_start(bd_sb[:], bd)
+
+        identity = held.tile([P, P], BF16, name="identity")
+        make_identity(nc, identity[:])
+
+        out_ps = psum.tile([E, N], F32, name="out_ps")
+
+        for h in range(H):
+            k_bf = held.tile([D, MW], BF16, name=f"k_bf{h}")
+            nc.vector.tensor_tensor(k_bf[:], key_sb[h][:], cal_sb[h][:], ADD)
+
+            q_ps = psum.tile([D, N], F32, name=f"q_ps{h}")
+            nc.tensor.matmul(
+                q_ps[:], wq_sb[:, h * D : (h + 1) * D], x_sb[:].indirect(offsets[:]), start=True, stop=True
+            )
+            q_bf = held.tile([D, N], BF16, name=f"q_bf{h}")
+            nc.vector.tensor_scalar(q_bf[:], q_ps[:], bq_sb[h][:, 0:1], None, ADD)
+
+            score_ps = psum.tile([P, JB, MW], F32, name=f"score_ps{h}")
+            for jb in range(JB):
+                nc.tensor.matmul(score_ps[:, jb, :], q_bf[:, jb * P : (jb + 1) * P], k_bf[:], start=True, stop=True)
+
+            top = held.tile([P, JB], F32, name=f"top{h}")
+            nc.vector.tensor_reduce(top[:], score_ps[:], mybir.AxisListType.X, MAX)
+            shift = held.tile([P, JB], F32, name=f"shift{h}")
+            nc.vector.tensor_scalar(shift[:], top[:], -SCALE, None, MULT)
+            expo = held.tile([P, JB, MW], F32, name=f"expo{h}")
+            total = held.tile([P, JB], F32, name=f"total{h}")
+            for jb in range(JB):
+                nc.scalar.activation(
+                    expo[:, jb, :],
+                    score_ps[:, jb, :],
+                    EXP,
+                    bias=shift[:, jb : jb + 1],
+                    scale=SCALE,
+                    accum_out=total[:, jb : jb + 1],
+                )
+            inverse = held.tile([P, JB], F32, name=f"inverse{h}")
+            nc.vector.reciprocal(inverse[:], total[:])
+            attn = held.tile([P, JB, MW], BF16, name=f"attn{h}")
+            for jb in range(JB):
+                nc.vector.tensor_scalar(attn[:, jb, :], expo[:, jb, :], inverse[:, jb : jb + 1], None, MULT)
+
+            attn_t_ps = psum.tile([P, MB, N], BF16, name=f"attn_t_ps{h}")
+            for jb in range(JB):
+                for mb in range(MB):
+                    nc.tensor.transpose(
+                        attn_t_ps[:, mb, jb * P : (jb + 1) * P], attn[:, jb, mb * P : (mb + 1) * P], identity[:]
+                    )
+            attn_t = held.tile([P, MB, N], BF16, name=f"attn_t{h}")
+            nc.vector.tensor_copy(attn_t[:], attn_t_ps[:])
+            for mb in range(MB):
+                nc.tensor.matmul(
+                    out_ps[:],
+                    value_sb[:, h * MB + mb, :],
+                    attn_t[:, mb, :],
+                    start=(h == 0 and mb == 0),
+                    stop=(h == H - 1 and mb == MB - 1),
+                )
+
+        out_sb = held.tile([E, N], F32, name="out_sb")
+        nc.vector.tensor_scalar(out_sb[:], out_ps[:], bd_sb[:, 0:1], None, ADD)
+        nc.sync.dma_start(out, out_sb[:])

@@ -5,7 +5,7 @@ from concourse.masks import make_identity
 
 BF16, F32, U16 = mybir.dt.bfloat16, mybir.dt.float32, mybir.dt.uint16
 ADD, MULT, MAX = mybir.AluOpType.add, mybir.AluOpType.mult, mybir.AluOpType.max
-EXP = mybir.ActivationFunctionType.Exp
+EXP, IDENTITY = mybir.ActivationFunctionType.Exp, mybir.ActivationFunctionType.Identity
 
 P = 128
 E, S, N, H, D, MW = 128, 256, 256, 2, 128, 256
@@ -20,85 +20,77 @@ def tile_autocalibrationinjector_kernel(tc, x, wq, bq, key_params, calibration, 
     nc = tc.nc
     with (
         tc.tile_pool(name="held", bufs=1) as held,
-        tc.psum_pool(name="psum", bufs=1) as psum,
+        tc.tile_pool(name="work", bufs=H * JB) as work,
+        tc.psum_pool(name="score_banks", bufs=H * JB) as score_banks,
+        tc.psum_pool(name="out_banks", bufs=1) as out_banks,
+        tc.psum_pool(name="turn_banks", bufs=2) as turn_banks,
     ):
-        offsets = held.tile([P, N // 16], U16, name="offsets")
-        nc.sync.dma_start(offsets[:], offs)
         x_sb = held.tile([E, S], BF16, name="x_sb")
         nc.sync.dma_start(x_sb[:], x)
+        offsets = held.tile([P, N // 16], U16, name="offsets")
+        nc.sync.dma_start(offsets[:], offs)
         wq_sb = held.tile([E, H * D], BF16, name="wq_sb")
         nc.scalar.dma_start(wq_sb[:], wq)
-        bq_sb = [held.tile([D, 1], F32, name=f"bq_sb{h}") for h in range(H)]
-        for h in range(H):
-            nc.scalar.dma_start(bq_sb[h][:], bq[h * D : (h + 1) * D, :])
+        bq_sb = held.tile([D, H], F32, name="bq_sb")
+        with nc.allow_non_contiguous_dma(reason="256 biases, one to a partition for each head"):
+            nc.scalar.dma_start(bq_sb[:], bq.rearrange("(h d) o -> d (h o)", d=D))
         key_sb = [held.tile([D, MW], F32, name=f"key_sb{h}") for h in range(H)]
         cal_sb = [held.tile([D, MW], F32, name=f"cal_sb{h}") for h in range(H)]
         for h in range(H):
             nc.sync.dma_start(key_sb[h][:], key_params[h * D : (h + 1) * D, :])
             nc.scalar.dma_start(cal_sb[h][:], calibration[h * D : (h + 1) * D, :])
         value_sb = held.tile([P, H * MB, E], BF16, name="value_sb")
-        nc.gpsimd.dma_start(value_sb[:], value.rearrange("(c m) e -> m c e", m=P))
+        nc.sync.dma_start(value_sb[:], value.rearrange("(c m) e -> m c e", m=P))
         bd_sb = held.tile([E, 1], F32, name="bd_sb")
-        nc.gpsimd.dma_start(bd_sb[:], bd)
+        nc.sync.dma_start(bd_sb[:], bd)
 
         identity = held.tile([P, P], BF16, name="identity")
         make_identity(nc, identity[:])
 
-        out_ps = psum.tile([E, N], F32, name="out_ps")
-
+        q_bf = [held.tile([D, N], BF16, name=f"q_bf{h}") for h in range(H)]
+        k_bf = [held.tile([D, MW], BF16, name=f"k_bf{h}") for h in range(H)]
         for h in range(H):
-            k_bf = held.tile([D, MW], BF16, name=f"k_bf{h}")
-            nc.vector.tensor_tensor(k_bf[:], key_sb[h][:], cal_sb[h][:], ADD)
-
-            q_ps = psum.tile([D, N], F32, name=f"q_ps{h}")
+            q_ps = turn_banks.tile([D, N], F32, name="q_ps", tag="turn")
             nc.tensor.matmul(
                 q_ps[:], wq_sb[:, h * D : (h + 1) * D], x_sb[:].indirect(offsets[:]), start=True, stop=True
             )
-            q_bf = held.tile([D, N], BF16, name=f"q_bf{h}")
-            nc.vector.tensor_scalar(q_bf[:], q_ps[:], bq_sb[h][:, 0:1], None, ADD)
+            nc.scalar.activation(q_bf[h][:], q_ps[:], IDENTITY, bias=bq_sb[:, h : h + 1])
+            nc.vector.tensor_tensor(k_bf[h][:], key_sb[h][:], cal_sb[h][:], ADD)
 
-            score_ps = psum.tile([P, JB, MW], F32, name=f"score_ps{h}")
-            for jb in range(JB):
-                nc.tensor.matmul(score_ps[:, jb, :], q_bf[:, jb * P : (jb + 1) * P], k_bf[:], start=True, stop=True)
+        out_ps = [out_banks.tile([E, P], F32, name=f"out_ps{jb}") for jb in range(JB)]
 
-            top = held.tile([P, JB], F32, name=f"top{h}")
-            nc.vector.tensor_reduce(top[:], score_ps[:], mybir.AxisListType.X, MAX)
-            shift = held.tile([P, JB], F32, name=f"shift{h}")
-            nc.vector.tensor_scalar(shift[:], top[:], -SCALE, None, MULT)
-            expo = held.tile([P, JB, MW], F32, name=f"expo{h}")
-            total = held.tile([P, JB], F32, name=f"total{h}")
+        for h in range(H):
             for jb in range(JB):
-                nc.scalar.activation(
-                    expo[:, jb, :],
-                    score_ps[:, jb, :],
-                    EXP,
-                    bias=shift[:, jb : jb + 1],
-                    scale=SCALE,
-                    accum_out=total[:, jb : jb + 1],
-                )
-            inverse = held.tile([P, JB], F32, name=f"inverse{h}")
-            nc.vector.reciprocal(inverse[:], total[:])
-            attn = held.tile([P, JB, MW], BF16, name=f"attn{h}")
-            for jb in range(JB):
-                nc.vector.tensor_scalar(attn[:, jb, :], expo[:, jb, :], inverse[:, jb : jb + 1], None, MULT)
+                score_ps = score_banks.tile([P, MW], F32, name="score_ps")
+                nc.tensor.matmul(score_ps[:], q_bf[h][:, jb * P : (jb + 1) * P], k_bf[h][:], start=True, stop=True)
 
-            attn_t_ps = psum.tile([P, MB, N], BF16, name=f"attn_t_ps{h}")
-            for jb in range(JB):
+                top = work.tile([P, 1], F32, name="top")
+                nc.vector.tensor_reduce(top[:], score_ps[:], mybir.AxisListType.X, MAX)
+                shift = work.tile([P, 1], F32, name="shift")
+                nc.vector.tensor_scalar(shift[:], top[:], -SCALE, None, MULT)
+                expo = work.tile([P, MW], F32, name="expo")
+                total = work.tile([P, 1], F32, name="total")
+                nc.scalar.activation(expo[:], score_ps[:], EXP, bias=shift[:, 0:1], scale=SCALE, accum_out=total[:])
+                inverse = work.tile([P, 1], F32, name="inverse")
+                nc.vector.reciprocal(inverse[:], total[:])
+                attn = work.tile([P, MW], BF16, name="attn")
+                nc.vector.tensor_scalar(attn[:], expo[:], inverse[:, 0:1], None, MULT)
+
+                attn_t_ps = turn_banks.tile([P, MB, P], BF16, name="attn_t_ps", tag="turn")
                 for mb in range(MB):
-                    nc.tensor.transpose(
-                        attn_t_ps[:, mb, jb * P : (jb + 1) * P], attn[:, jb, mb * P : (mb + 1) * P], identity[:]
+                    nc.tensor.transpose(attn_t_ps[:, mb, :], attn[:, mb * P : (mb + 1) * P], identity[:])
+                attn_t = work.tile([P, MB, P], BF16, name="attn_t")
+                nc.scalar.copy(attn_t[:], attn_t_ps[:])
+                for mb in range(MB):
+                    nc.tensor.matmul(
+                        out_ps[jb][:],
+                        value_sb[:, h * MB + mb, :],
+                        attn_t[:, mb, :],
+                        start=(h == 0 and mb == 0),
+                        stop=(h == H - 1 and mb == MB - 1),
                     )
-            attn_t = held.tile([P, MB, N], BF16, name=f"attn_t{h}")
-            nc.vector.tensor_copy(attn_t[:], attn_t_ps[:])
-            for mb in range(MB):
-                nc.tensor.matmul(
-                    out_ps[:],
-                    value_sb[:, h * MB + mb, :],
-                    attn_t[:, mb, :],
-                    start=(h == 0 and mb == 0),
-                    stop=(h == H - 1 and mb == MB - 1),
-                )
 
-        out_sb = held.tile([E, N], F32, name="out_sb")
-        nc.vector.tensor_scalar(out_sb[:], out_ps[:], bd_sb[:, 0:1], None, ADD)
-        nc.sync.dma_start(out, out_sb[:])
+        for jb in range(JB):
+            out_sb = work.tile([E, P], F32, name="out_sb")
+            nc.vector.tensor_scalar(out_sb[:], out_ps[jb][:], bd_sb[:, 0:1], None, ADD)
+            nc.sync.dma_start(out[:, jb * P : (jb + 1) * P], out_sb[:])

@@ -4,7 +4,7 @@ import concourse.mybir as mybir
 from concourse.masks import make_identity
 
 BF16, F32, U16 = mybir.dt.bfloat16, mybir.dt.float32, mybir.dt.uint16
-ADD, MULT, MAX = mybir.AluOpType.add, mybir.AluOpType.mult, mybir.AluOpType.max
+ADD, MULT, MIN = mybir.AluOpType.add, mybir.AluOpType.mult, mybir.AluOpType.min
 EXP, IDENTITY = mybir.ActivationFunctionType.Exp, mybir.ActivationFunctionType.Identity
 
 P = 128
@@ -44,6 +44,11 @@ def tile_autocalibrationinjector_kernel(tc, x, wq, bq, key_params, calibration, 
         bd_sb = held.tile([E, 1], F32, name="bd_sb")
         nc.sync.dma_start(bd_sb[:], bd)
 
+        zero = held.tile([P, 1], F32, name="zero")
+        nc.gpsimd.memset(zero[:], 0.0)
+        unused = held.tile([P, 1], F32, name="unused")
+        nc.scalar.activation(unused[:], zero[:], EXP)
+
         identity = held.tile([P, P], BF16, name="identity")
         make_identity(nc, identity[:])
 
@@ -64,13 +69,12 @@ def tile_autocalibrationinjector_kernel(tc, x, wq, bq, key_params, calibration, 
                 score_ps = score_banks.tile([P, MW], F32, name="score_ps")
                 nc.tensor.matmul(score_ps[:], q_bf[h][:, jb * P : (jb + 1) * P], k_bf[h][:], start=True, stop=True)
 
-                top = work.tile([P, 1], F32, name="top")
-                nc.vector.tensor_reduce(top[:], score_ps[:], mybir.AxisListType.X, MAX)
+                negated = work.tile([P, MW], F32, name="negated")
                 shift = work.tile([P, 1], F32, name="shift")
-                nc.vector.tensor_scalar(shift[:], top[:], -SCALE, None, MULT)
+                nc.vector.tensor_scalar(negated[:], score_ps[:], -SCALE, None, MULT, MIN, accum_out=shift[:])
                 expo = work.tile([P, MW], F32, name="expo")
                 total = work.tile([P, 1], F32, name="total")
-                nc.scalar.activation(expo[:], score_ps[:], EXP, bias=shift[:, 0:1], scale=SCALE, accum_out=total[:])
+                nc.scalar.activation(expo[:], negated[:], EXP, bias=shift[:, 0:1], scale=-1.0, accum_out=total[:])
                 inverse = work.tile([P, 1], F32, name="inverse")
                 nc.vector.reciprocal(inverse[:], total[:])
                 attn = work.tile([P, MW], BF16, name="attn")

@@ -13,6 +13,8 @@ JB = N // P
 MB = MW // P
 SCALE = 1.0 / math.sqrt(E)
 
+WARM_MATMULS = 11
+
 FLOPS = 2 * E * H * D * N + 2 * H * D * MW * N + 2 * H * MW * E * N
 
 
@@ -51,6 +53,10 @@ def tile_autocalibrationinjector_kernel(tc, x, wq, bq, key_params, calibration, 
 
         identity = held.tile([P, P], BF16, name="identity")
         make_identity(nc, identity[:])
+
+        warm_ps = turn_banks.tile([P, P], F32, name="warm_ps", tag="turn")
+        for i in range(WARM_MATMULS):
+            nc.tensor.matmul(warm_ps[:], identity[:], identity[:], start=True, stop=True)
 
         q_bf = [held.tile([D, N], BF16, name=f"q_bf{h}") for h in range(H)]
         k_bf = [held.tile([D, MW], BF16, name=f"k_bf{h}") for h in range(H)]

@@ -13,7 +13,8 @@ JB = N // P
 MB = MW // P
 SCALE = 1.0 / math.sqrt(E)
 
-WARM_MATMULS = 11
+WARM_MATMULS = 8
+WARM_COLUMNS = 128
 
 FLOPS = 2 * E * H * D * N + 2 * H * D * MW * N + 2 * H * MW * E * N
 
@@ -47,16 +48,18 @@ def tile_autocalibrationinjector_kernel(tc, x, wq, bq, key_params, calibration, 
         nc.sync.dma_start(bd_sb[:], bd)
 
         zero = held.tile([P, 1], F32, name="zero")
-        nc.gpsimd.memset(zero[:], 0.0)
+        nc.vector.memset(zero[:], 0.0)
         unused = held.tile([P, 1], F32, name="unused")
         nc.scalar.activation(unused[:], zero[:], EXP)
 
+        zeros = held.tile([P, WARM_COLUMNS], BF16, name="zeros")
+        nc.vector.memset(zeros[:], 0.0)
+        warm_ps = turn_banks.tile([P, WARM_COLUMNS], F32, name="warm_ps", tag="turn")
+        for i in range(WARM_MATMULS):
+            nc.tensor.matmul(warm_ps[:], zeros[:, 0:P], zeros[:], start=True, stop=True)
+
         identity = held.tile([P, P], BF16, name="identity")
         make_identity(nc, identity[:])
-
-        warm_ps = turn_banks.tile([P, P], F32, name="warm_ps", tag="turn")
-        for i in range(WARM_MATMULS):
-            nc.tensor.matmul(warm_ps[:], identity[:], identity[:], start=True, stop=True)
 
         q_bf = [held.tile([D, N], BF16, name=f"q_bf{h}") for h in range(H)]
         k_bf = [held.tile([D, MW], BF16, name=f"k_bf{h}") for h in range(H)]
@@ -70,27 +73,32 @@ def tile_autocalibrationinjector_kernel(tc, x, wq, bq, key_params, calibration, 
 
         out_ps = [out_banks.tile([E, P], F32, name=f"out_ps{jb}") for jb in range(JB)]
 
+        expos = [[work.tile([P, MW], F32, name=f"expo{h}_{jb}", tag="expo") for jb in range(JB)] for h in range(H)]
+        totals = [held.tile([P, JB], F32, name=f"totals{h}") for h in range(H)]
         for h in range(H):
             for jb in range(JB):
-                score_ps = score_banks.tile([P, MW], F32, name="score_ps")
+                score_ps = score_banks.tile([P, MW], F32, name="score_ps", tag="unit")
                 nc.tensor.matmul(score_ps[:], q_bf[h][:, jb * P : (jb + 1) * P], k_bf[h][:], start=True, stop=True)
 
                 negated = work.tile([P, MW], F32, name="negated")
                 shift = work.tile([P, 1], F32, name="shift")
                 nc.vector.tensor_scalar(negated[:], score_ps[:], -SCALE, None, MULT, MIN, accum_out=shift[:])
-                expo = work.tile([P, MW], F32, name="expo")
-                total = work.tile([P, 1], F32, name="total")
-                nc.scalar.activation(expo[:], negated[:], EXP, bias=shift[:, 0:1], scale=-1.0, accum_out=total[:])
-                inverse = work.tile([P, 1], F32, name="inverse")
-                nc.vector.reciprocal(inverse[:], total[:])
-                attn = work.tile([P, MW], BF16, name="attn")
-                nc.vector.tensor_scalar(attn[:], expo[:], inverse[:, 0:1], None, MULT)
+                nc.scalar.activation(
+                    expos[h][jb][:], negated[:], EXP, bias=shift[:, 0:1], scale=-1.0, accum_out=totals[h][:, jb : jb + 1]
+                )
 
-                attn_t_ps = turn_banks.tile([P, MB, P], BF16, name="attn_t_ps", tag="turn")
+        for h in range(H):
+            inverses = work.tile([P, JB], F32, name="inverses")
+            nc.vector.reciprocal(inverses[:], totals[h][:])
+            for jb in range(JB):
+                attn = work.tile([P, MW], BF16, name="attn")
+                nc.vector.tensor_scalar(attn[:], expos[h][jb][:], inverses[:, jb : jb + 1], None, MULT)
+
+                attn_t_ps = score_banks.tile([P, MB, P], BF16, name="attn_t_ps", tag="unit")
                 for mb in range(MB):
                     nc.tensor.transpose(attn_t_ps[:, mb, :], attn[:, mb * P : (mb + 1) * P], identity[:])
                 attn_t = work.tile([P, MB, P], BF16, name="attn_t")
-                nc.scalar.copy(attn_t[:], attn_t_ps[:])
+                nc.vector.tensor_copy(attn_t[:], attn_t_ps[:])
                 for mb in range(MB):
                     nc.tensor.matmul(
                         out_ps[jb][:],

@@ -13,7 +13,8 @@ JB = N // P
 MB = MW // P
 SCALE = 1.0 / math.sqrt(E)
 
-WARM_MATMULS = 8
+WARM_MATMULS = 12
+MID_MATMULS = 8
 WARM_COLUMNS = 128
 
 FLOPS = 2 * E * H * D * N + 2 * H * D * MW * N + 2 * H * MW * E * N
@@ -86,6 +87,10 @@ def tile_autocalibrationinjector_kernel(tc, x, wq, bq, key_params, calibration, 
                 nc.scalar.activation(
                     expos[h][jb][:], negated[:], EXP, bias=shift[:, 0:1], scale=-1.0, accum_out=totals[h][:, jb : jb + 1]
                 )
+
+        mid_ps = score_banks.tile([P, WARM_COLUMNS], F32, name="mid_ps", tag="unit")
+        for i in range(MID_MATMULS):
+            nc.tensor.matmul(mid_ps[:], zeros[:, 0:P], zeros[:], start=True, stop=True)
 
         for h in range(H):
             inverses = work.tile([P, JB], F32, name="inverses")

@@ -14,7 +14,7 @@ MB = MW // P
 SCALE = 1.0 / math.sqrt(E)
 
 WARM_MATMULS = 12
-MID_MATMULS = 8
+MID_MATMULS = 16
 WARM_COLUMNS = 128
 
 FLOPS = 2 * E * H * D * N + 2 * H * D * MW * N + 2 * H * MW * E * N

@@ -13,7 +13,7 @@ JB = N // P
 MB = MW // P
 SCALE = 1.0 / math.sqrt(E)
 
-WARM_MATMULS = 12
+WARM_MATMULS = 13
 MID_MATMULS = 16
 WARM_COLUMNS = 128
 
@@ -48,13 +48,14 @@ def tile_autocalibrationinjector_kernel(tc, x, wq, bq, key_params, calibration, 
         bd_sb = held.tile([E, 1], F32, name="bd_sb")
         nc.sync.dma_start(bd_sb[:], bd)
 
+        zeros = held.tile([P, WARM_COLUMNS], BF16, name="zeros")
+        nc.vector.memset(zeros[:], 0.0)
         zero = held.tile([P, 1], F32, name="zero")
         nc.vector.memset(zero[:], 0.0)
+
         unused = held.tile([P, 1], F32, name="unused")
         nc.scalar.activation(unused[:], zero[:], EXP)
 
-        zeros = held.tile([P, WARM_COLUMNS], BF16, name="zeros")
-        nc.vector.memset(zeros[:], 0.0)
         warm_ps = turn_banks.tile([P, WARM_COLUMNS], F32, name="warm_ps", tag="turn")
         for i in range(WARM_MATMULS):
             nc.tensor.matmul(warm_ps[:], zeros[:, 0:P], zeros[:], start=True, stop=True)
@@ -62,14 +63,15 @@ def tile_autocalibrationinjector_kernel(tc, x, wq, bq, key_params, calibration, 
         identity = held.tile([P, P], BF16, name="identity")
         make_identity(nc, identity[:])
 
-        q_bf = [held.tile([D, N], BF16, name=f"q_bf{h}") for h in range(H)]
+        q_bf = [[held.tile([D, P], BF16, name=f"q_bf{h}_{jb}") for jb in range(JB)] for h in range(H)]
         k_bf = [held.tile([D, MW], BF16, name=f"k_bf{h}") for h in range(H)]
         for h in range(H):
             q_ps = turn_banks.tile([D, N], F32, name="q_ps", tag="turn")
             nc.tensor.matmul(
                 q_ps[:], wq_sb[:, h * D : (h + 1) * D], x_sb[:].indirect(offsets[:]), start=True, stop=True
             )
-            nc.scalar.activation(q_bf[h][:], q_ps[:], IDENTITY, bias=bq_sb[:, h : h + 1])
+            for jb in range(JB):
+                nc.scalar.activation(q_bf[h][jb][:], q_ps[:, jb * P : (jb + 1) * P], IDENTITY, bias=bq_sb[:, h : h + 1])
             nc.vector.tensor_tensor(k_bf[h][:], key_sb[h][:], cal_sb[h][:], ADD)
 
         out_ps = [out_banks.tile([E, P], F32, name=f"out_ps{jb}") for jb in range(JB)]
@@ -79,7 +81,7 @@ def tile_autocalibrationinjector_kernel(tc, x, wq, bq, key_params, calibration, 
         for h in range(H):
             for jb in range(JB):
                 score_ps = score_banks.tile([P, MW], F32, name="score_ps", tag="unit")
-                nc.tensor.matmul(score_ps[:], q_bf[h][:, jb * P : (jb + 1) * P], k_bf[h][:], start=True, stop=True)
+                nc.tensor.matmul(score_ps[:], q_bf[h][jb][:], k_bf[h][:], start=True, stop=True)
 
                 negated = work.tile([P, MW], F32, name="negated")
                 shift = work.tile([P, 1], F32, name="shift")

@@ -26,8 +26,7 @@ def tile_autocalibrationinjector_kernel(tc, x, wq, bq, key_params, calibration, 
         tc.tile_pool(name="held", bufs=1) as held,
         tc.tile_pool(name="work", bufs=H * JB) as work,
         tc.psum_pool(name="score_banks", bufs=H * JB) as score_banks,
-        tc.psum_pool(name="out_banks", bufs=1) as out_banks,
-        tc.psum_pool(name="turn_banks", bufs=2) as turn_banks,
+        tc.psum_pool(name="turn_banks", bufs=H * JB) as turn_banks,
     ):
         x_sb = held.tile([E, S], BF16, name="x_sb")
         nc.sync.dma_start(x_sb[:], x)
@@ -74,25 +73,27 @@ def tile_autocalibrationinjector_kernel(tc, x, wq, bq, key_params, calibration, 
                 nc.scalar.activation(q_bf[h][jb][:], q_ps[:, jb * P : (jb + 1) * P], IDENTITY, bias=bq_sb[:, h : h + 1])
             nc.vector.tensor_tensor(k_bf[h][:], key_sb[h][:], cal_sb[h][:], ADD)
 
-        out_ps = [out_banks.tile([E, P], F32, name=f"out_ps{jb}") for jb in range(JB)]
-
         expos = [[work.tile([P, MW], F32, name=f"expo{h}_{jb}", tag="expo") for jb in range(JB)] for h in range(H)]
         totals = [held.tile([P, JB], F32, name=f"totals{h}") for h in range(H)]
         for h in range(H):
             for jb in range(JB):
+                rough_ps = turn_banks.tile([P, MW], BF16, name="rough_ps", tag="turn")
+                nc.tensor.matmul(rough_ps[:], q_bf[h][jb][:], k_bf[h][:], start=True, stop=True)
                 score_ps = score_banks.tile([P, MW], F32, name="score_ps", tag="unit")
                 nc.tensor.matmul(score_ps[:], q_bf[h][jb][:], k_bf[h][:], start=True, stop=True)
 
-                negated = work.tile([P, MW], F32, name="negated")
+                negated = work.tile([P, MW], BF16, name="negated")
                 shift = work.tile([P, 1], F32, name="shift")
-                nc.vector.tensor_scalar(negated[:], score_ps[:], -SCALE, None, MULT, MIN, accum_out=shift[:])
+                nc.vector.tensor_scalar(negated[:], rough_ps[:], -SCALE, None, MULT, MIN, accum_out=shift[:])
                 nc.scalar.activation(
-                    expos[h][jb][:], negated[:], EXP, bias=shift[:, 0:1], scale=-1.0, accum_out=totals[h][:, jb : jb + 1]
+                    expos[h][jb][:], score_ps[:], EXP, bias=shift[:, 0:1], scale=SCALE, accum_out=totals[h][:, jb : jb + 1]
                 )
 
-        mid_ps = score_banks.tile([P, WARM_COLUMNS], F32, name="mid_ps", tag="unit")
+        mid_ps = turn_banks.tile([P, WARM_COLUMNS], F32, name="mid_ps", tag="turn")
         for i in range(MID_MATMULS):
             nc.tensor.matmul(mid_ps[:], zeros[:, 0:P], zeros[:], start=True, stop=True)
+
+        out_ps = [turn_banks.tile([E, P], F32, name=f"out_ps{jb}", tag="turn") for jb in range(JB)]
 
         for h in range(H):
             inverses = work.tile([P, JB], F32, name="inverses")

@@ -11,6 +11,7 @@ P = 128
 E, S, N, H, D, MW = 128, 256, 256, 2, 128, 256
 JB = N // P
 MB = MW // P
+BLOCK = 32
 SCALE = 1.0 / math.sqrt(E)
 
 WARM_MATMULS = 13
@@ -34,14 +35,18 @@ def tile_autocalibrationinjector_kernel(tc, x, wq, bq, key_params, calibration, 
         nc.sync.dma_start(offsets[:], offs)
         wq_sb = held.tile([E, H * D], BF16, name="wq_sb")
         nc.scalar.dma_start(wq_sb[:], wq)
-        bq_sb = held.tile([D, H], F32, name="bq_sb")
-        with nc.allow_non_contiguous_dma(reason="256 biases, one to a partition for each head"):
-            nc.scalar.dma_start(bq_sb[:], bq.rearrange("(h d) o -> d (h o)", d=D))
         key_sb = [held.tile([D, MW], F32, name=f"key_sb{h}") for h in range(H)]
         cal_sb = [held.tile([D, MW], F32, name=f"cal_sb{h}") for h in range(H)]
+        bq_blocks = held.tile([D, H * BLOCK], F32, name="bq_blocks", align_bytes=64)
+        nc.gpsimd.memset(bq_blocks[:], 0.0)
         for h in range(H):
             nc.sync.dma_start(key_sb[h][:], key_params[h * D : (h + 1) * D, :])
             nc.scalar.dma_start(cal_sb[h][:], calibration[h * D : (h + 1) * D, :])
+            if h == 0:
+                nc.scalar.dma_start(
+                    bq_blocks[::BLOCK, :].rearrange("b (h i) -> b h i", h=H),
+                    bq.rearrange("(h b i) o -> b h (i o)", h=H, i=BLOCK),
+                )
         value_sb = held.tile([P, H * MB, E], BF16, name="value_sb")
         nc.sync.dma_start(value_sb[:], value.rearrange("(c m) e -> m c e", m=P))
         bd_sb = held.tile([E, 1], F32, name="bd_sb")
@@ -62,6 +67,11 @@ def tile_autocalibrationinjector_kernel(tc, x, wq, bq, key_params, calibration, 
         identity = held.tile([P, P], BF16, name="identity")
         make_identity(nc, identity[:])
 
+        bq_columns = held.tile([D, H * BLOCK], F32, name="bq_columns", align_bytes=64)
+        for h in range(H):
+            head = slice(h * BLOCK, (h + 1) * BLOCK)
+            nc.vector.transpose(bq_columns[:, head], bq_blocks[:, head])
+
         q_bf = [[held.tile([D, P], BF16, name=f"q_bf{h}_{jb}") for jb in range(JB)] for h in range(H)]
         k_bf = [held.tile([D, MW], BF16, name=f"k_bf{h}") for h in range(H)]
         for h in range(H):
@@ -70,7 +80,7 @@ def tile_autocalibrationinjector_kernel(tc, x, wq, bq, key_params, calibration, 
                 q_ps[:], wq_sb[:, h * D : (h + 1) * D], x_sb[:].indirect(offsets[:]), start=True, stop=True
             )
             for jb in range(JB):
-                nc.scalar.activation(q_bf[h][jb][:], q_ps[:, jb * P : (jb + 1) * P], IDENTITY, bias=bq_sb[:, h : h + 1])
+                nc.scalar.activation(q_bf[h][jb][:], q_ps[:, jb * P : (jb + 1) * P], IDENTITY, bias=bq_columns[:, h * BLOCK : h * BLOCK + 1])
             nc.vector.tensor_tensor(k_bf[h][:], key_sb[h][:], cal_sb[h][:], ADD)
 
         expos = [[work.tile([P, MW], F32, name=f"expo{h}_{jb}", tag="expo") for jb in range(JB)] for h in range(H)]

import math

import concourse.mybir as mybir
from concourse.masks import make_identity

BF16, F32, U16 = mybir.dt.bfloat16, mybir.dt.float32, mybir.dt.uint16
ADD, MULT, MIN = mybir.AluOpType.add, mybir.AluOpType.mult, mybir.AluOpType.min
EXP, IDENTITY = mybir.ActivationFunctionType.Exp, mybir.ActivationFunctionType.Identity

P = 128
E, S, N, H, D, MW = 128, 256, 256, 2, 128, 256
JB = N // P
MB = MW // P
BLOCK = 32
SCALE = 1.0 / math.sqrt(E)

WARM_MATMULS = 13
MID_MATMULS = 16
WARM_COLUMNS = 128

FLOPS = 2 * E * H * D * N + 2 * H * D * MW * N + 2 * H * MW * E * N


def tile_autocalibrationinjector_kernel(tc, x, wq, bq, key_params, calibration, value, bd, offs, out):
    nc = tc.nc
    with (
        tc.tile_pool(name="held", bufs=1) as held,
        tc.tile_pool(name="work", bufs=H * JB) as work,
        tc.psum_pool(name="score_banks", bufs=H * JB) as score_banks,
        tc.psum_pool(name="turn_banks", bufs=H * JB) as turn_banks,
    ):
        x_sb = held.tile([E, S], BF16, name="x_sb")
        nc.sync.dma_start(x_sb[:], x)
        offsets = held.tile([P, N // 16], U16, name="offsets")
        nc.sync.dma_start(offsets[:], offs)
        wq_sb = held.tile([E, H * D], BF16, name="wq_sb")
        nc.scalar.dma_start(wq_sb[:], wq)
        key_sb = [held.tile([D, MW], F32, name=f"key_sb{h}") for h in range(H)]
        cal_sb = [held.tile([D, MW], F32, name=f"cal_sb{h}") for h in range(H)]
        bq_blocks = held.tile([D, H * BLOCK], F32, name="bq_blocks", align_bytes=64)
        nc.gpsimd.memset(bq_blocks[:], 0.0)
        for h in range(H):
            nc.sync.dma_start(key_sb[h][:], key_params[h * D : (h + 1) * D, :])
            nc.scalar.dma_start(cal_sb[h][:], calibration[h * D : (h + 1) * D, :])
            if h == 0:
                nc.scalar.dma_start(
                    bq_blocks[::BLOCK, :].rearrange("b (h i) -> b h i", h=H),
                    bq.rearrange("(h b i) o -> b h (i o)", h=H, i=BLOCK),
                )
        value_sb = held.tile([P, H * MB, E], BF16, name="value_sb")
        nc.sync.dma_start(value_sb[:], value.rearrange("(c m) e -> m c e", m=P))
        bd_sb = held.tile([E, 1], F32, name="bd_sb")
        nc.sync.dma_start(bd_sb[:], bd)

        zeros = held.tile([P, WARM_COLUMNS], BF16, name="zeros")
        nc.vector.memset(zeros[:], 0.0)
        zero = held.tile([P, 1], F32, name="zero")
        nc.vector.memset(zero[:], 0.0)

        unused = held.tile([P, 1], F32, name="unused")
        nc.scalar.activation(unused[:], zero[:], EXP)

        warm_ps = turn_banks.tile([P, WARM_COLUMNS], F32, name="warm_ps", tag="turn")
        for i in range(WARM_MATMULS):
            nc.tensor.matmul(warm_ps[:], zeros[:, 0:P], zeros[:], start=True, stop=True)

        identity = held.tile([P, P], BF16, name="identity")
        make_identity(nc, identity[:])

        bq_columns = held.tile([D, H * BLOCK], F32, name="bq_columns", align_bytes=64)
        for h in range(H):
            head = slice(h * BLOCK, (h + 1) * BLOCK)
            nc.vector.transpose(bq_columns[:, head], bq_blocks[:, head])

        q_bf = [[held.tile([D, P], BF16, name=f"q_bf{h}_{jb}") for jb in range(JB)] for h in range(H)]
        k_bf = [held.tile([D, MW], BF16, name=f"k_bf{h}") for h in range(H)]
        for h in range(H):
            q_ps = turn_banks.tile([D, N], F32, name="q_ps", tag="turn")
            nc.tensor.matmul(
                q_ps[:], wq_sb[:, h * D : (h + 1) * D], x_sb[:].indirect(offsets[:]), start=True, stop=True
            )
            for jb in range(JB):
                nc.scalar.activation(q_bf[h][jb][:], q_ps[:, jb * P : (jb + 1) * P], IDENTITY, bias=bq_columns[:, h * BLOCK : h * BLOCK + 1])
            nc.vector.tensor_tensor(k_bf[h][:], key_sb[h][:], cal_sb[h][:], ADD)

        expos = [[work.tile([P, MW], F32, name=f"expo{h}_{jb}", tag="expo") for jb in range(JB)] for h in range(H)]
        totals = [held.tile([P, JB], F32, name=f"totals{h}") for h in range(H)]
        for h in range(H):
            for jb in range(JB):
                rough_ps = turn_banks.tile([P, MW], BF16, name="rough_ps", tag="turn")
                nc.tensor.matmul(rough_ps[:], q_bf[h][jb][:], k_bf[h][:], start=True, stop=True)
                score_ps = score_banks.tile([P, MW], F32, name="score_ps", tag="unit")
                nc.tensor.matmul(score_ps[:], q_bf[h][jb][:], k_bf[h][:], start=True, stop=True)

                negated = work.tile([P, MW], BF16, name="negated")
                shift = work.tile([P, 1], F32, name="shift")
                nc.vector.tensor_scalar(negated[:], rough_ps[:], -SCALE, None, MULT, MIN, accum_out=shift[:])
                nc.scalar.activation(
                    expos[h][jb][:], score_ps[:], EXP, bias=shift[:, 0:1], scale=SCALE, accum_out=totals[h][:, jb : jb + 1]
                )

        mid_ps = turn_banks.tile([P, WARM_COLUMNS], F32, name="mid_ps", tag="turn")
        for i in range(MID_MATMULS):
            nc.tensor.matmul(mid_ps[:], zeros[:, 0:P], zeros[:], start=True, stop=True)

        out_ps = [turn_banks.tile([E, P], F32, name=f"out_ps{jb}", tag="turn") for jb in range(JB)]

        for h in range(H):
            inverses = work.tile([P, JB], F32, name="inverses")
            nc.vector.reciprocal(inverses[:], totals[h][:])
            for jb in range(JB):
                attn = work.tile([P, MW], BF16, name="attn")
                nc.vector.tensor_scalar(attn[:], expos[h][jb][:], inverses[:, jb : jb + 1], None, MULT)

                attn_t_ps = score_banks.tile([P, MB, P], BF16, name="attn_t_ps", tag="unit")
                for mb in range(MB):
                    nc.tensor.transpose(attn_t_ps[:, mb, :], attn[:, mb * P : (mb + 1) * P], identity[:])
                attn_t = work.tile([P, MB, P], BF16, name="attn_t")
                nc.vector.tensor_copy(attn_t[:], attn_t_ps[:])
                for mb in range(MB):
                    nc.tensor.matmul(
                        out_ps[jb][:],
                        value_sb[:, h * MB + mb, :],
                        attn_t[:, mb, :],
                        start=(h == 0 and mb == 0),
                        stop=(h == H - 1 and mb == MB - 1),
                    )

        for jb in range(JB):
            out_sb = work.tile([E, P], F32, name="out_sb")
            nc.vector.tensor_scalar(out_sb[:], out_ps[jb][:], bd_sb[:, 0:1], None, ADD)
            nc.sync.dma_start(out[:, jb * P : (jb + 1) * P], out_sb[:])
